import numpy as np
import ml_dtypes


def mxq(x, axis, fmt="e4m3"):
    dtype, down = {"e4m3": (ml_dtypes.float8_e4m3fn, 7), "e5m2": (ml_dtypes.float8_e5m2, 14)}[fmt]
    v = np.moveaxis(np.asarray(x, np.float32).astype(ml_dtypes.bfloat16).astype(np.float64), axis, -1)
    blocks = v.reshape(v.shape[:-1] + (-1, 32))
    amax = np.abs(blocks).max(-1, keepdims=True)
    byte = np.maximum(np.where(amax > 0, np.frexp(amax)[1] - 1 + 127, 0) - down, 1)
    scale = np.exp2(byte - 127.0)
    codes = (blocks / scale).astype(np.float32).astype(dtype).astype(np.float64)
    return np.moveaxis((codes * scale).reshape(v.shape), -1, axis)


WIDE = False


def mx_kscale(k):
    if not WIDE:
        return np.ones(k)
    levels = np.array([20, -20, 10, -10, 0])
    a = np.random.permutation(np.resize(levels, k // 512 * 4)).reshape(k // 512, 4)
    idx = np.arange(k)
    return np.exp2(a[idx // 512, idx % 128 // 32])


BF16 = ml_dtypes.bfloat16


def bf(x):
    return np.asarray(x, np.float32).astype(BF16)


def f64(x):
    return np.asarray(x).astype(np.float64)


BATCH, IN_FEATURES, OUT_BY_WIN, WIN_SIZE, STRIDE = 4096, 512, 32, 64, 16
N_WIN = -(-IN_FEATURES // STRIDE)
OUT_FEATURES = N_WIN * OUT_BY_WIN


def build_mask():
    offset = WIN_SIZE // 2
    k = np.arange(N_WIN)
    lo = np.maximum(k * STRIDE - offset, 0)
    hi = k * STRIDE + WIN_SIZE - offset
    j = np.arange(IN_FEATURES)
    win_mask = (j[None, :] >= lo[:, None]) & (j[None, :] < hi[:, None])
    return np.repeat(win_mask, OUT_BY_WIN, axis=0).astype(np.float64)


def setup_inputs():
    u = mx_kscale(OUT_FEATURES)
    mask = build_mask()
    bound = np.sqrt(3.0 / WIN_SIZE)
    W = np.random.uniform(-bound, bound, (OUT_FEATURES, IN_FEATURES)) * mask
    x = np.random.standard_normal((BATCH, IN_FEATURES))
    b = np.random.uniform(-0.5, 0.5, OUT_FEATURES)
    g = np.random.standard_normal((BATCH, OUT_FEATURES)) * np.exp2(np.random.randint(-12, 1, (BATCH, 1))) * 8.0
    return {"x": bf(x), "W": bf(W / u[:, None]), "b": bf(b), "mask": bf(mask),
            "grad_out": bf(g * u[None, :])}


def reference(x, W, b, mask, grad_out):
    return mxq(f64(grad_out), 1, "e5m2") @ mxq(f64(W), 0, "e4m3")

@@ -1,0 +1,164 @@
+from contextlib import ExitStack
+
+import concourse.mybir as mybir
+from concourse.masks import make_identity
+
+BF16 = mybir.dt.bfloat16
+F32 = mybir.dt.float32
+U32 = mybir.dt.uint32
+U8 = mybir.dt.uint8
+E5X4 = mybir.dt.float8_e5m2_x4
+E4X4 = mybir.dt.float8_e4m3fn_x4
+
+P = 128
+BATCH, K, N = 4096, 1024, 512
+NT = BATCH // P
+G = 4
+NG = NT // G
+CW = 288
+W_C0 = (0, N - CW)
+
+FLOPS = 2 * BATCH * K * N
+BYTES = BATCH * K * 2 + 63488 * 2 + BATCH * N * 4
+
+LOADS = (1, 1, 1, 1) + (4,) * 7
+
+
+def tile_locallayer_t_kernel(tc, x, W, b, mask, grad_out, out):
+    nc = tc.nc
+    gx = grad_out.rearrange("(p t) k -> p t k", t=NT)
+    ox = out.rearrange("(p t) n -> p t n", t=NT)
+    with ExitStack() as ctx:
+        const = ctx.enter_context(tc.tile_pool(name="const", bufs=1))
+        xin = ctx.enter_context(tc.tile_pool(name="xin", bufs=1))
+        grp = ctx.enter_context(tc.tile_pool(name="grp", bufs=3))
+        res = ctx.enter_context(tc.tile_pool(name="res", bufs=1))
+        psum = ctx.enter_context(tc.psum_pool(name="psum", bufs=1))
+        ctx.enter_context(tc.manual_schedule())
+
+        ident = const.tile([P, P], F32, name="ident")
+        make_identity(nc, ident[:])
+        w_raw = [const.tile([P, 4, CW], BF16, name="w_raw%d" % g) for g in range(2)]
+        w_grp = [const.tile([P, 4 * N], BF16, name="w_grp%d" % g, align_bytes=64) for g in range(2)]
+        w_codes = const.tile([P, 2 * N], U32, name="w_codes", align_bytes=64)
+        w_scales = const.tile([P, 2 * N], U8, name="w_scales", align_bytes=64)
+        nc.vector.memset(w_grp[0][:, 4 * CW:], 0.0)
+        nc.vector.memset(w_grp[1][:, : 4 * (N - CW)], 0.0)
+
+        for g in range(2):
+            for u in range(2):
+                r0 = 512 * g + 256 * u
+                nc.sync.dma_start(
+                    out=w_raw[g][:, 2 * u: 2 * u + 2, :],
+                    in_=W[r0: r0 + 256, W_C0[g]: W_C0[g] + CW].rearrange("(q e) c -> q e c", e=2),
+                )
+        x_of = {}
+        t0 = 0
+        for n in LOADS:
+            xt = xin.tile([P, n, K], BF16, name="x%d" % t0)
+            nc.sync.dma_start(out=xt[:], in_=gx[:, t0: t0 + n, :])
+            for j in range(n):
+                x_of[t0 + j] = xt[:, j, :]
+            t0 += n
+
+        for g in range(2):
+            dst = w_grp[g][:, 4 * W_C0[g]: 4 * (W_C0[g] + CW)].rearrange("p (c i t) -> p c t i", i=4, t=4)
+            src = w_raw[g][:].rearrange("p t (c i) -> p c t i", i=4)
+            if g == 0:
+                nc.vector.tensor_copy(out=dst, in_=src)
+            else:
+                nc.scalar.copy(out=dst, in_=src)
+        for g in range(2):
+            nc.vector.quantize_mx(
+                out=w_codes[:, N * g: N * (g + 1)].bitcast(E4X4),
+                scales=w_scales[:, N * g: N * (g + 1)],
+                in_=w_grp[g][:],
+            )
+
+        state = {}
+
+        def transposes(i):
+            banks = []
+            for j in range(G):
+                tp = psum.tile([P, 4, P], F32, name="tp%d_%d" % (i, j), tag="tp%d" % j)
+                words = x_of[G * i + j].bitcast(F32)
+                for q in range(4):
+                    nc.tensor.transpose(tp[:, q, :], words[:, P * q: P * (q + 1)], ident[:])
+                banks.append(tp)
+            grouped = grp.tile([P, G * K], BF16, name="grouped%d" % i, tag="grouped", align_bytes=64)
+            codes = grp.tile([P, G * K // 4], U32, name="codes%d" % i, tag="codes", align_bytes=64)
+            scales = grp.tile([P, G * K // 4], U8, name="scales%d" % i, tag="scales", align_bytes=64)
+            state[i] = (banks, grouped, codes, scales)
+
+        def copy_t(i, j, eng):
+            banks, grouped, codes, scales = state[i]
+            dst = grouped[:, K * j: K * (j + 1)].bitcast(F32).rearrange("p (g c u) -> p g c u", g=2, u=2)
+            src = banks[j][:].rearrange("p (g u) c -> p g c u", u=2)
+            if eng == 0:
+                nc.vector.tensor_copy(out=dst, in_=src)
+            else:
+                nc.scalar.copy(out=dst, in_=src)
+
+        def quantise(i, h):
+            banks, grouped, codes, scales = state[i]
+            w = G * K // 2
+            nc.vector.quantize_mx(
+                out=codes[:, (w // 4) * h: (w // 4) * (h + 1)].bitcast(E5X4),
+                scales=scales[:, (w // 4) * h: (w // 4) * (h + 1)],
+                in_=grouped[:, w * h: w * (h + 1)],
+            )
+
+        def passes(i):
+            banks, grouped, codes, scales = state[i]
+            accs = []
+            for j in range(G):
+                acc = psum.tile([P, N], F32, name="acc%d_%d" % (i, j), tag="acc%d" % j)
+                for g in range(2):
+                    c0 = 256 * j + P * g
+                    nc.tensor.matmul_mx(
+                        out=acc[:],
+                        lhsT=codes[:, c0: c0 + P].bitcast(E5X4),
+                        lhsT_scale=scales[:, c0: c0 + P],
+                        rhs=w_codes[:, N * g: N * (g + 1)].bitcast(E4X4),
+                        rhs_scale=w_scales[:, N * g: N * (g + 1)],
+                        start=(g == 0),
+                        stop=(g == 1),
+                    )
+                accs.append(acc)
+            o_sb = res.tile([P, G, N], F32, name="o%d" % i)
+            return accs, o_sb
+
+        def evac(accs, o_sb, j, eng):
+            if eng == 0:
+                nc.vector.tensor_copy(out=o_sb[:, j, :], in_=accs[j][:])
+            else:
+                nc.scalar.copy(out=o_sb[:, j, :], in_=accs[j][:])
+
+        def prepare_head(i):
+            transposes(i)
+            copy_t(i, 0, 0)
+            copy_t(i, 1, 1)
+            copy_t(i, 2, 0)
+            copy_t(i, 3, 1)
+            quantise(i, 0)
+
+        prepare_head(0)
+        quantise(0, 1)
+        for i in range(NG):
+            last = i == NG - 1
+            if not last:
+                prepare_head(i + 1)
+            accs, o_sb = passes(i)
+            evac(accs, o_sb, 0, 0)
+            if not last:
+                quantise(i + 1, 1)
+                evac(accs, o_sb, 1, 1)
+                evac(accs, o_sb, 2, 1)
+                evac(accs, o_sb, 3, 1)
+                nc.sync.dma_start(out=ox[:, G * i: G * (i + 1), :], in_=o_sb[:])
+            else:
+                evac(accs, o_sb, 1, 1)
+                nc.sync.dma_start(out=ox[:, G * i: G * i + 2, :], in_=o_sb[:, 0:2, :])
+                evac(accs, o_sb, 2, 0)
+                evac(accs, o_sb, 3, 1)
+                nc.sync.dma_start(out=ox[:, G * i + 2: G * i + 4, :], in_=o_sb[:, 2:4, :])

@@ -5,6 +5,7 @@ from concourse.masks import make_identity
 
 BF16 = mybir.dt.bfloat16
 F32 = mybir.dt.float32
+I32 = mybir.dt.int32
 U32 = mybir.dt.uint32
 U8 = mybir.dt.uint8
 E5X4 = mybir.dt.float8_e5m2_x4
@@ -13,15 +14,20 @@ E4X4 = mybir.dt.float8_e4m3fn_x4
 P = 128
 BATCH, K, N = 4096, 1024, 512
 NT = BATCH // P
-G = 4
-NG = NT // G
 CW = 288
 W_C0 = (0, N - CW)
 
 FLOPS = 2 * BATCH * K * N
 BYTES = BATCH * K * 2 + 63488 * 2 + BATCH * N * 4
 
-LOADS = (1, 1, 1, 1) + (4,) * 7
+T_GROUPS = (4,) * 8
+M_GROUPS = (2, 2) + (4,) * 7
+Q_UNITS = (1, 1, 2) + (2,) * 14
+LOADS = (1, 1, 2, 4, 4, 4, 8, 8)
+STORES = (8, 8, 4, 4, 4, 1, 1, 1, 1)
+DUMMIES = 0
+DUMMIES_BETWEEN = 0
+VEC, ACT = 0, 1
 
 
 def tile_locallayer_t_kernel(tc, x, W, b, mask, grad_out, out):
@@ -31,7 +37,7 @@ def tile_locallayer_t_kernel(tc, x, W, b, mask, grad_out, out):
     with ExitStack() as ctx:
         const = ctx.enter_context(tc.tile_pool(name="const", bufs=1))
         xin = ctx.enter_context(tc.tile_pool(name="xin", bufs=1))
-        grp = ctx.enter_context(tc.tile_pool(name="grp", bufs=3))
+        grp = ctx.enter_context(tc.tile_pool(name="grp", bufs=6))
         res = ctx.enter_context(tc.tile_pool(name="res", bufs=1))
         psum = ctx.enter_context(tc.psum_pool(name="psum", bufs=1))
         ctx.enter_context(tc.manual_schedule())
@@ -42,8 +48,28 @@ def tile_locallayer_t_kernel(tc, x, W, b, mask, grad_out, out):
         w_grp = [const.tile([P, 4 * N], BF16, name="w_grp%d" % g, align_bytes=64) for g in range(2)]
         w_codes = const.tile([P, 2 * N], U32, name="w_codes", align_bytes=64)
         w_scales = const.tile([P, 2 * N], U8, name="w_scales", align_bytes=64)
+        if DUMMIES or DUMMIES_BETWEEN:
+            d_codes = const.tile([P, N], U32, name="d_codes", align_bytes=64)
+            d_scales = const.tile([P, N], U8, name="d_scales", align_bytes=64)
+            nc.vector.memset(d_codes[:].bitcast(I32), 0)
+            nc.vector.memset(d_scales[:].bitcast(I32), 0)
         nc.vector.memset(w_grp[0][:, 4 * CW:], 0.0)
         nc.vector.memset(w_grp[1][:, : 4 * (N - CW)], 0.0)
+
+        def dummies(n, tag):
+            if n == 0:
+                return
+            waste = psum.tile([P, N], F32, name="waste_" + tag, tag="acc3")
+            for d in range(n):
+                nc.tensor.matmul_mx(
+                    out=waste[:],
+                    lhsT=d_codes[:, :P].bitcast(E5X4),
+                    lhsT_scale=d_scales[:, :P],
+                    rhs=d_codes[:].bitcast(E4X4),
+                    rhs_scale=d_scales[:],
+                    start=True,
+                    stop=True,
+                )
 
         for g in range(2):
             for u in range(2):
@@ -60,6 +86,17 @@ def tile_locallayer_t_kernel(tc, x, W, b, mask, grad_out, out):
             for j in range(n):
                 x_of[t0 + j] = xt[:, j, :]
             t0 += n
+        o_of = {}
+        store_after = {}
+        t0 = 0
+        for n in STORES:
+            ot = res.tile([P, n, N], F32, name="o%d" % t0)
+            for j in range(n):
+                o_of[t0 + j] = ot[:, j, :]
+            store_after[t0 + n - 1] = (ot, t0, n)
+            t0 += n
+
+        dummies(DUMMIES, "head")
 
         for g in range(2):
             dst = w_grp[g][:, 4 * W_C0[g]: 4 * (W_C0[g] + CW)].rearrange("p (c i t) -> p c t i", i=4, t=4)
@@ -75,90 +112,106 @@ def tile_locallayer_t_kernel(tc, x, W, b, mask, grad_out, out):
                 in_=w_grp[g][:],
             )
 
-        state = {}
+        def firsts(sizes):
+            return [sum(sizes[:i]) for i in range(len(sizes))]
 
-        def transposes(i):
-            banks = []
-            for j in range(G):
-                tp = psum.tile([P, 4, P], F32, name="tp%d_%d" % (i, j), tag="tp%d" % j)
-                words = x_of[G * i + j].bitcast(F32)
-                for q in range(4):
-                    nc.tensor.transpose(tp[:, q, :], words[:, P * q: P * (q + 1)], ident[:])
-                banks.append(tp)
-            grouped = grp.tile([P, G * K], BF16, name="grouped%d" % i, tag="grouped", align_bytes=64)
-            codes = grp.tile([P, G * K // 4], U32, name="codes%d" % i, tag="codes", align_bytes=64)
-            scales = grp.tile([P, G * K // 4], U8, name="scales%d" % i, tag="scales", align_bytes=64)
-            state[i] = (banks, grouped, codes, scales)
+        t_first, m_first, q_first = firsts(T_GROUPS), firsts(M_GROUPS), firsts(Q_UNITS)
+        unit_of = {}
+        for iq in range(len(Q_UNITS)):
+            for j in range(Q_UNITS[iq]):
+                unit_of[q_first[iq] + j] = (iq, j)
+        banks = {}
+        units = {}
 
-        def copy_t(i, j, eng):
-            banks, grouped, codes, scales = state[i]
-            dst = grouped[:, K * j: K * (j + 1)].bitcast(F32).rearrange("p (g c u) -> p g c u", g=2, u=2)
-            src = banks[j][:].rearrange("p (g u) c -> p g c u", u=2)
-            if eng == 0:
+        def copy(eng, dst, src):
+            if eng == VEC:
                 nc.vector.tensor_copy(out=dst, in_=src)
             else:
                 nc.scalar.copy(out=dst, in_=src)
 
-        def quantise(i, h):
-            banks, grouped, codes, scales = state[i]
-            w = G * K // 2
-            nc.vector.quantize_mx(
-                out=codes[:, (w // 4) * h: (w // 4) * (h + 1)].bitcast(E5X4),
-                scales=scales[:, (w // 4) * h: (w // 4) * (h + 1)],
-                in_=grouped[:, w * h: w * (h + 1)],
-            )
+        def transpose(t):
+            tp = psum.tile([P, 4, P], F32, name="tp%d" % t, tag="tp%d" % (t % 4))
+            words = x_of[t].bitcast(F32)
+            for q in range(4):
+                nc.tensor.transpose(tp[:, q, :], words[:, P * q: P * (q + 1)], ident[:])
+            banks[t] = tp
 
-        def passes(i):
-            banks, grouped, codes, scales = state[i]
-            accs = []
-            for j in range(G):
-                acc = psum.tile([P, N], F32, name="acc%d_%d" % (i, j), tag="acc%d" % j)
-                for g in range(2):
-                    c0 = 256 * j + P * g
-                    nc.tensor.matmul_mx(
-                        out=acc[:],
-                        lhsT=codes[:, c0: c0 + P].bitcast(E5X4),
-                        lhsT_scale=scales[:, c0: c0 + P],
-                        rhs=w_codes[:, N * g: N * (g + 1)].bitcast(E4X4),
-                        rhs_scale=w_scales[:, N * g: N * (g + 1)],
-                        start=(g == 0),
-                        stop=(g == 1),
-                    )
-                accs.append(acc)
-            o_sb = res.tile([P, G, N], F32, name="o%d" % i)
-            return accs, o_sb
+        def copy_t(t, eng):
+            iq, j = unit_of[t]
+            if iq not in units:
+                n = Q_UNITS[iq]
+                grouped = grp.tile([P, n * K], BF16, name="grouped%d" % iq, tag="grouped", align_bytes=64)
+                codes = grp.tile([P, n * K // 4], U32, name="codes%d" % iq, tag="codes", align_bytes=64)
+                scales = grp.tile([P, n * K // 4], U8, name="scales%d" % iq, tag="scales", align_bytes=64)
+                units[iq] = (grouped, codes, scales)
+            grouped = units[iq][0]
+            dst = grouped[:, K * j: K * (j + 1)].bitcast(F32).rearrange("p (g c u) -> p g c u", g=2, u=2)
+            copy(eng, dst, banks[t][:].rearrange("p (g u) c -> p g c u", u=2))
 
-        def evac(accs, o_sb, j, eng):
-            if eng == 0:
-                nc.vector.tensor_copy(out=o_sb[:, j, :], in_=accs[j][:])
+        def quantise(t):
+            grouped, codes, scales = units[unit_of[t][0]]
+            nc.vector.quantize_mx(out=codes[:].bitcast(E5X4), scales=scales[:], in_=grouped[:])
+
+        accs = {}
+
+        def multiply(t):
+            iq, j = unit_of[t]
+            grouped, codes, scales = units[iq]
+            acc = psum.tile([P, N], F32, name="acc%d" % t, tag="acc%d" % (t % 4))
+            for g in range(2):
+                c0 = 256 * j + P * g
+                nc.tensor.matmul_mx(
+                    out=acc[:],
+                    lhsT=codes[:, c0: c0 + P].bitcast(E5X4),
+                    lhsT_scale=scales[:, c0: c0 + P],
+                    rhs=w_codes[:, N * g: N * (g + 1)].bitcast(E4X4),
+                    rhs_scale=w_scales[:, N * g: N * (g + 1)],
+                    start=(g == 0),
+                    stop=(g == 1),
+                )
+            accs[t] = acc
+
+        def evac(t, eng):
+            copy(eng, o_of[t], accs[t][:])
+            if t in store_after:
+                ot, s0, n = store_after[t]
+                nc.sync.dma_start(out=ox[:, s0: s0 + n, :], in_=ot[:])
+
+        for t in range(4):
+            transpose(t)
+            if t < 3:
+                dummies(DUMMIES_BETWEEN, "b%d" % t)
+        copy_t(0, ACT)
+        quantise(0)
+        copy_t(1, ACT)
+        quantise(1)
+        copy_t(2, VEC)
+        copy_t(3, ACT)
+        quantise(2)
+        nm = len(M_GROUPS)
+        for im in range(nm):
+            late = None
+            if 1 <= im < len(T_GROUPS):
+                a = t_first[im]
+                for t in range(a, a + 4):
+                    transpose(t)
+                copy_t(a, VEC)
+                copy_t(a + 1, ACT)
+                copy_t(a + 2, VEC)
+                copy_t(a + 3, ACT)
+                quantise(a)
+                late = a + 2
+            m0, n = m_first[im], M_GROUPS[im]
+            for t in range(m0, m0 + n):
+                multiply(t)
+            if im == nm - 1:
+                engines = (VEC, ACT, VEC, ACT)
+            elif im == 0:
+                engines = (ACT, ACT)
             else:
-                nc.scalar.copy(out=o_sb[:, j, :], in_=accs[j][:])
-
-        def prepare_head(i):
-            transposes(i)
-            copy_t(i, 0, 0)
-            copy_t(i, 1, 1)
-            copy_t(i, 2, 0)
-            copy_t(i, 3, 1)
-            quantise(i, 0)
-
-        prepare_head(0)
-        quantise(0, 1)
-        for i in range(NG):
-            last = i == NG - 1
-            if not last:
-                prepare_head(i + 1)
-            accs, o_sb = passes(i)
-            evac(accs, o_sb, 0, 0)
-            if not last:
-                quantise(i + 1, 1)
-                evac(accs, o_sb, 1, 1)
-                evac(accs, o_sb, 2, 1)
-                evac(accs, o_sb, 3, 1)
-                nc.sync.dma_start(out=ox[:, G * i: G * (i + 1), :], in_=o_sb[:])
-            else:
-                evac(accs, o_sb, 1, 1)
-                nc.sync.dma_start(out=ox[:, G * i: G * i + 2, :], in_=o_sb[:, 0:2, :])
-                evac(accs, o_sb, 2, 0)
-                evac(accs, o_sb, 3, 1)
-                nc.sync.dma_start(out=ox[:, G * i + 2: G * i + 4, :], in_=o_sb[:, 2:4, :])
+                engines = (VEC, ACT, ACT, ACT)
+            evac(m0, engines[0])
+            if late is not None:
+                quantise(late)
+            for j in range(1, n):
+                evac(m0 + j, engines[j])

@@ -14,8 +14,8 @@ E4X4 = mybir.dt.float8_e4m3fn_x4
 P = 128
 BATCH, K, N = 4096, 1024, 512
 NT = BATCH // P
-CW = 288
-W_C0 = (0, N - CW)
+W_SPAN = 320
+W_BASE = (0, N - W_SPAN)
 
 FLOPS = 2 * BATCH * K * N
 BYTES = BATCH * K * 2 + 63488 * 2 + BATCH * N * 4
@@ -44,8 +44,16 @@ def tile_locallayer_t_kernel(tc, x, W, b, mask, grad_out, out):
 
         ident = const.tile([P, P], F32, name="ident")
         make_identity(nc, ident[:])
-        w_raw = [const.tile([P, 4, CW], BF16, name="w_raw%d" % g) for g in range(2)]
-        w_grp = [const.tile([P, 4 * N], BF16, name="w_grp%d" % g, align_bytes=64) for g in range(2)]
+        def w_live(g, u):
+            c = 256 * g + 128 * u
+            return max(c - 32, 0), min(c + 144, N)
+
+        w_raw = {}
+        for g in range(2):
+            for u in range(2):
+                lo, hi = w_live(g, u)
+                w_raw[(g, u)] = const.tile([P, 2, hi - lo], BF16, name="w_raw%d%d" % (g, u))
+        w_grp = [const.tile([P, 4 * W_SPAN], BF16, name="w_grp%d" % g, align_bytes=64) for g in range(2)]
         w_codes = const.tile([P, 2 * N], U32, name="w_codes", align_bytes=64)
         w_scales = const.tile([P, 2 * N], U8, name="w_scales", align_bytes=64)
         if DUMMIES or DUMMIES_BETWEEN:
@@ -53,8 +61,10 @@ def tile_locallayer_t_kernel(tc, x, W, b, mask, grad_out, out):
             d_scales = const.tile([P, N], U8, name="d_scales", align_bytes=64)
             nc.vector.memset(d_codes[:].bitcast(I32), 0)
             nc.vector.memset(d_scales[:].bitcast(I32), 0)
-        nc.vector.memset(w_grp[0][:, 4 * CW:], 0.0)
-        nc.vector.memset(w_grp[1][:, : 4 * (N - CW)], 0.0)
+        nc.vector.memset(w_grp[0][:], 0.0)
+        nc.vector.memset(w_grp[1][:], 0.0)
+        nc.vector.memset(w_codes[:, W_SPAN: N + W_BASE[1]].bitcast(I32), 0)
+        nc.vector.memset(w_scales[:, W_SPAN: N + W_BASE[1]].bitcast(I32), 0)
 
         def dummies(n, tag):
             if n == 0:
@@ -74,9 +84,10 @@ def tile_locallayer_t_kernel(tc, x, W, b, mask, grad_out, out):
         for g in range(2):
             for u in range(2):
                 r0 = 512 * g + 256 * u
+                lo, hi = w_live(g, u)
                 nc.sync.dma_start(
-                    out=w_raw[g][:, 2 * u: 2 * u + 2, :],
-                    in_=W[r0: r0 + 256, W_C0[g]: W_C0[g] + CW].rearrange("(q e) c -> q e c", e=2),
+                    out=w_raw[(g, u)][:],
+                    in_=W[r0: r0 + 256, lo:hi].rearrange("(q e) c -> q e c", e=2),
                 )
         x_of = {}
         t0 = 0
@@ -99,18 +110,22 @@ def tile_locallayer_t_kernel(tc, x, W, b, mask, grad_out, out):
         dummies(DUMMIES, "head")
 
         for g in range(2):
-            dst = w_grp[g][:, 4 * W_C0[g]: 4 * (W_C0[g] + CW)].rearrange("p (c i t) -> p c t i", i=4, t=4)
-            src = w_raw[g][:].rearrange("p t (c i) -> p c t i", i=4)
-            if g == 0:
-                nc.vector.tensor_copy(out=dst, in_=src)
-            else:
-                nc.scalar.copy(out=dst, in_=src)
-        for g in range(2):
-            nc.vector.quantize_mx(
-                out=w_codes[:, N * g: N * (g + 1)].bitcast(E4X4),
-                scales=w_scales[:, N * g: N * (g + 1)],
-                in_=w_grp[g][:],
-            )
+            for u in range(2):
+                lo, hi = w_live(g, u)
+                dst = w_grp[g][:].rearrange("p (c t) -> p c t", t=4)[:, lo - W_BASE[g]: hi - W_BASE[g], 2 * u: 2 * u + 2]
+                src = w_raw[(g, u)][:].rearrange("p e c -> p c e")
+                if g == 0:
+                    nc.vector.tensor_copy(out=dst, in_=src)
+                else:
+                    nc.scalar.copy(out=dst, in_=src)
+        for g, cuts in ((0, (0, 256, 320)), (1, (0, 64, 320))):
+            for lo, hi in zip(cuts[:-1], cuts[1:]):
+                c0 = N * g + W_BASE[g]
+                nc.vector.quantize_mx(
+                    out=w_codes[:, c0 + lo: c0 + hi].bitcast(E4X4),
+                    scales=w_scales[:, c0 + lo: c0 + hi],
+                    in_=w_grp[g][:, 4 * lo: 4 * hi],
+                )
 
         def firsts(sizes):
             return [sum(sizes[:i]) for i in range(len(sizes))]

@@ -25,8 +25,6 @@ M_GROUPS = (2, 2) + (4,) * 7
 Q_UNITS = (1, 1, 2) + (2,) * 14
 LOADS = (1, 1, 2, 4, 4, 4, 8, 8)
 STORES = (8, 8, 4, 4, 4, 1, 1, 1, 1)
-DUMMIES = 0
-DUMMIES_BETWEEN = 0
 VEC, ACT = 0, 1
 
 
@@ -56,44 +54,39 @@ def tile_locallayer_t_kernel(tc, x, W, b, mask, grad_out, out):
         w_grp = [const.tile([P, 4 * W_SPAN], BF16, name="w_grp%d" % g, align_bytes=64) for g in range(2)]
         w_codes = const.tile([P, 2 * N], U32, name="w_codes", align_bytes=64)
         w_scales = const.tile([P, 2 * N], U8, name="w_scales", align_bytes=64)
-        if DUMMIES or DUMMIES_BETWEEN:
-            d_codes = const.tile([P, N], U32, name="d_codes", align_bytes=64)
-            d_scales = const.tile([P, N], U8, name="d_scales", align_bytes=64)
-            nc.vector.memset(d_codes[:].bitcast(I32), 0)
-            nc.vector.memset(d_scales[:].bitcast(I32), 0)
+        zeros = const.tile([P, N], BF16, name="zeros")
+        nc.vector.memset(zeros[:], 0.0)
+        warm = const.tile([P, 8], F32, name="warm")
+        warm_out = const.tile([P, 8], F32, name="warm_out")
+        nc.vector.memset(warm[:], 0.0)
+        nc.scalar.copy(out=warm_out[:], in_=warm[:])
         nc.vector.memset(w_grp[0][:], 0.0)
         nc.vector.memset(w_grp[1][:], 0.0)
         nc.vector.memset(w_codes[:, W_SPAN: N + W_BASE[1]].bitcast(I32), 0)
         nc.vector.memset(w_scales[:, W_SPAN: N + W_BASE[1]].bitcast(I32), 0)
 
         def dummies(n, tag):
-            if n == 0:
-                return
             waste = psum.tile([P, N], F32, name="waste_" + tag, tag="acc3")
             for d in range(n):
-                nc.tensor.matmul_mx(
-                    out=waste[:],
-                    lhsT=d_codes[:, :P].bitcast(E5X4),
-                    lhsT_scale=d_scales[:, :P],
-                    rhs=d_codes[:].bitcast(E4X4),
-                    rhs_scale=d_scales[:],
-                    start=True,
-                    stop=True,
-                )
+                nc.tensor.matmul(waste[:], lhsT=zeros[:, :P], rhs=zeros[:], start=True, stop=True)
 
-        for g in range(2):
-            for u in range(2):
-                r0 = 512 * g + 256 * u
-                lo, hi = w_live(g, u)
-                nc.sync.dma_start(
-                    out=w_raw[(g, u)][:],
-                    in_=W[r0: r0 + 256, lo:hi].rearrange("(q e) c -> q e c", e=2),
-                )
+        def load_w():
+            for g in range(2):
+                for u in range(2):
+                    r0 = 512 * g + 256 * u
+                    lo, hi = w_live(g, u)
+                    nc.sync.dma_start(
+                        out=w_raw[(g, u)][:],
+                        in_=W[r0: r0 + 256, lo:hi].rearrange("(q e) c -> q e c", e=2),
+                    )
+
         x_of = {}
         t0 = 0
         for n in LOADS:
             xt = xin.tile([P, n, K], BF16, name="x%d" % t0)
             nc.sync.dma_start(out=xt[:], in_=gx[:, t0: t0 + n, :])
+            if t0 == 0:
+                load_w()
             for j in range(n):
                 x_of[t0 + j] = xt[:, j, :]
             t0 += n
@@ -107,9 +100,9 @@ def tile_locallayer_t_kernel(tc, x, W, b, mask, grad_out, out):
             store_after[t0 + n - 1] = (ot, t0, n)
             t0 += n
 
-        dummies(DUMMIES, "head")
+        dummies(4, "a")
 
-        for g in range(2):
+        def group_w(g):
             for u in range(2):
                 lo, hi = w_live(g, u)
                 dst = w_grp[g][:].rearrange("p (c t) -> p c t", t=4)[:, lo - W_BASE[g]: hi - W_BASE[g], 2 * u: 2 * u + 2]
@@ -118,7 +111,9 @@ def tile_locallayer_t_kernel(tc, x, W, b, mask, grad_out, out):
                     nc.vector.tensor_copy(out=dst, in_=src)
                 else:
                     nc.scalar.copy(out=dst, in_=src)
-        for g, cuts in ((0, (0, 256, 320)), (1, (0, 64, 320))):
+
+        def quantise_w(g):
+            cuts = ((0, 256, 320), (0, 64, 320))[g]
             for lo, hi in zip(cuts[:-1], cuts[1:]):
                 c0 = N * g + W_BASE[g]
                 nc.vector.quantize_mx(
@@ -192,19 +187,29 @@ def tile_locallayer_t_kernel(tc, x, W, b, mask, grad_out, out):
                 ot, s0, n = store_after[t]
                 nc.sync.dma_start(out=ox[:, s0: s0 + n, :], in_=ot[:])
 
-        for t in range(4):
-            transpose(t)
-            if t < 3:
-                dummies(DUMMIES_BETWEEN, "b%d" % t)
+        transpose(0)
         copy_t(0, ACT)
+        dummies(3, "b")
+        group_w(0)
         quantise(0)
+        group_w(1)
+        quantise_w(0)
+        transpose(1)
         copy_t(1, ACT)
+        dummies(1, "c")
+        quantise_w(1)
+        multiply(0)
         quantise(1)
+        transpose(2)
+        transpose(3)
         copy_t(2, VEC)
         copy_t(3, ACT)
+        multiply(1)
+        evac(0, ACT)
         quantise(2)
+        evac(1, ACT)
         nm = len(M_GROUPS)
-        for im in range(nm):
+        for im in range(1, nm):
             late = None
             if 1 <= im < len(T_GROUPS):
                 a = t_first[im]
@@ -221,8 +226,6 @@ def tile_locallayer_t_kernel(tc, x, W, b, mask, grad_out, out):
                 multiply(t)
             if im == nm - 1:
                 engines = (VEC, ACT, VEC, ACT)
-            elif im == 0:
-                engines = (ACT, ACT)
             else:
                 engines = (VEC, ACT, ACT, ACT)
             evac(m0, engines[0])

@@ -20,8 +20,7 @@ W_BASE = (0, N - W_SPAN)
 FLOPS = 2 * BATCH * K * N
 BYTES = BATCH * K * 2 + 63488 * 2 + BATCH * N * 4
 
-T_GROUPS = (4,) * 8
-M_GROUPS = (2, 2) + (4,) * 7
+RUNS = (4, 4, 8, 8, 4)
 Q_UNITS = (1, 1, 2) + (2,) * 14
 LOADS = (1, 1, 2, 4, 4, 4, 8, 8)
 STORES = (8, 8, 4, 4, 4, 1, 1, 1, 1)
@@ -35,7 +34,7 @@ def tile_locallayer_t_kernel(tc, x, W, b, mask, grad_out, out):
     with ExitStack() as ctx:
         const = ctx.enter_context(tc.tile_pool(name="const", bufs=1))
         xin = ctx.enter_context(tc.tile_pool(name="xin", bufs=1))
-        grp = ctx.enter_context(tc.tile_pool(name="grp", bufs=6))
+        grp = ctx.enter_context(tc.tile_pool(name="grp", bufs=10))
         res = ctx.enter_context(tc.tile_pool(name="res", bufs=1))
         psum = ctx.enter_context(tc.psum_pool(name="psum", bufs=1))
         ctx.enter_context(tc.manual_schedule())
@@ -125,7 +124,7 @@ def tile_locallayer_t_kernel(tc, x, W, b, mask, grad_out, out):
         def firsts(sizes):
             return [sum(sizes[:i]) for i in range(len(sizes))]
 
-        t_first, m_first, q_first = firsts(T_GROUPS), firsts(M_GROUPS), firsts(Q_UNITS)
+        q_first = firsts(Q_UNITS)
         unit_of = {}
         for iq in range(len(Q_UNITS)):
             for j in range(Q_UNITS[iq]):
@@ -208,28 +207,35 @@ def tile_locallayer_t_kernel(tc, x, W, b, mask, grad_out, out):
         evac(0, ACT)
         quantise(2)
         evac(1, ACT)
-        nm = len(M_GROUPS)
-        for im in range(1, nm):
-            late = None
-            if 1 <= im < len(T_GROUPS):
-                a = t_first[im]
-                for t in range(a, a + 4):
-                    transpose(t)
-                copy_t(a, VEC)
-                copy_t(a + 1, ACT)
-                copy_t(a + 2, VEC)
-                copy_t(a + 3, ACT)
-                quantise(a)
-                late = a + 2
-            m0, n = m_first[im], M_GROUPS[im]
-            for t in range(m0, m0 + n):
+
+        def matched(m_tiles, units):
+            for t in m_tiles:
                 multiply(t)
-            if im == nm - 1:
-                engines = (VEC, ACT, VEC, ACT)
-            else:
-                engines = (VEC, ACT, ACT, ACT)
-            evac(m0, engines[0])
-            if late is not None:
-                quantise(late)
-            for j in range(1, n):
-                evac(m0 + j, engines[j])
+            units = list(units)
+            for i, t in enumerate(m_tiles):
+                if i % 4 == 0:
+                    if units:
+                        quantise(units.pop(0))
+                    evac(t, VEC)
+                    if units:
+                        quantise(units.pop(0))
+                else:
+                    evac(t, ACT)
+            for t in units:
+                quantise(t)
+
+        last = range(2, 4)
+        a = 4
+        for n in RUNS:
+            tiles = range(a, a + n)
+            for t in tiles:
+                transpose(t)
+            for t in tiles:
+                copy_t(t, VEC if (t - a) % 2 == 0 else ACT)
+            matched(last, range(a, a + n, 2))
+            last = tiles
+            a += n
+        for t in last:
+            multiply(t)
+        for t in last:
+            evac(t, VEC if (t - last[0]) % 2 == 0 else ACT)

@@ -20,7 +20,7 @@ W_BASE = (0, N - W_SPAN)
 FLOPS = 2 * BATCH * K * N
 BYTES = BATCH * K * 2 + 63488 * 2 + BATCH * N * 4
 
-RUNS = (4, 4, 8, 8, 4)
+RUNS = (2,) * 14
 Q_UNITS = (1, 1, 2) + (2,) * 14
 LOADS = (1, 1, 2, 4, 4, 4, 8, 8)
 STORES = (8, 8, 4, 4, 4, 1, 1, 1, 1)
@@ -211,18 +211,10 @@ def tile_locallayer_t_kernel(tc, x, W, b, mask, grad_out, out):
         def matched(m_tiles, units):
             for t in m_tiles:
                 multiply(t)
-            units = list(units)
-            for i, t in enumerate(m_tiles):
-                if i % 4 == 0:
-                    if units:
-                        quantise(units.pop(0))
-                    evac(t, VEC)
-                    if units:
-                        quantise(units.pop(0))
-                else:
-                    evac(t, ACT)
             for t in units:
                 quantise(t)
+            for t in m_tiles:
+                evac(t, VEC if t % 4 == 0 else ACT)
 
         last = range(2, 4)
         a = 4

@@ -20,10 +20,10 @@ W_BASE = (0, N - W_SPAN)
 FLOPS = 2 * BATCH * K * N
 BYTES = BATCH * K * 2 + 63488 * 2 + BATCH * N * 4
 
-RUNS = (2,) * 14
+STEPS = ((2, 2), (4, 2)) + ((2, 2),) * 11
 Q_UNITS = (1, 1, 2) + (2,) * 14
-LOADS = (1, 1, 2, 4, 4, 4, 8, 8)
-STORES = (8, 8, 4, 4, 4, 1, 1, 1, 1)
+LOADS = (1, 1, 2, 2, 2, 4, 4, 8, 8)
+STORES = (8, 4, 4, 4, 2, 2, 2, 2, 1, 1, 1, 1)
 VEC, ACT = 0, 1
 
 
@@ -208,26 +208,28 @@ def tile_locallayer_t_kernel(tc, x, W, b, mask, grad_out, out):
         quantise(2)
         evac(1, ACT)
 
-        def matched(m_tiles, units):
-            for t in m_tiles:
-                multiply(t)
-            for t in units:
-                quantise(t)
-            for t in m_tiles:
-                evac(t, VEC if t % 4 == 0 else ACT)
+        def drain(t):
+            evac(t, VEC if t % 4 == 0 else ACT)
 
-        last = range(2, 4)
-        a = 4
-        for n in RUNS:
-            tiles = range(a, a + n)
-            for t in tiles:
+        t0, m0 = 4, 2
+        waiting = []
+        for i, (n_t, n_m) in enumerate(STEPS):
+            for t in range(t0, t0 + n_t):
                 transpose(t)
-            for t in tiles:
-                copy_t(t, VEC if (t - a) % 2 == 0 else ACT)
-            matched(last, range(a, a + n, 2))
-            last = tiles
-            a += n
-        for t in last:
+            for t in range(t0, t0 + n_t):
+                copy_t(t, VEC if t % 2 == 0 else ACT)
+            if waiting:
+                quantise(waiting.pop(0))
+            waiting.extend(range(t0, t0 + n_t, 2))
+            for t in range(m0, m0 + n_m):
+                multiply(t)
+            for t in range(m0, m0 + n_m):
+                drain(t)
+            while len(waiting) > min(i, 1):
+                quantise(waiting.pop(0))
+            t0, m0 = t0 + n_t, m0 + n_m
+        quantise(waiting[0])
+        for t in range(m0, NT):
             multiply(t)
-        for t in last:
-            evac(t, VEC if (t - last[0]) % 2 == 0 else ACT)
+        for t in range(m0, NT):
+            evac(t, VEC if t % 2 == 0 else ACT)

@@ -21,9 +21,9 @@ FLOPS = 2 * BATCH * K * N
 BYTES = BATCH * K * 2 + 63488 * 2 + BATCH * N * 4
 
 STEPS = ((2, 2), (4, 2)) + ((2, 2),) * 11
-Q_UNITS = (1, 1, 2) + (2,) * 14
-LOADS = (1, 1, 2, 2, 2, 4, 4, 8, 8)
-STORES = (8, 4, 4, 4, 2, 2, 2, 2, 1, 1, 1, 1)
+Q_UNITS = (1, 1, 1, 1) + (2,) * 14
+LOADS = (1, 1, 1, 1, 2, 2, 4, 4, 8, 8)
+STORES = (8, 4, 4, 4, 2, 2) + (1,) * 8
 VEC, ACT = 0, 1
 
 
@@ -106,7 +106,7 @@ def tile_locallayer_t_kernel(tc, x, W, b, mask, grad_out, out):
                 lo, hi = w_live(g, u)
                 dst = w_grp[g][:].rearrange("p (c t) -> p c t", t=4)[:, lo - W_BASE[g]: hi - W_BASE[g], 2 * u: 2 * u + 2]
                 src = w_raw[(g, u)][:].rearrange("p e c -> p c e")
-                if g == 0:
+                if g == 0 or u == 1:
                     nc.vector.tensor_copy(out=dst, in_=src)
                 else:
                     nc.scalar.copy(out=dst, in_=src)
@@ -191,21 +191,21 @@ def tile_locallayer_t_kernel(tc, x, W, b, mask, grad_out, out):
         dummies(3, "b")
         group_w(0)
         quantise(0)
-        group_w(1)
         quantise_w(0)
+        group_w(1)
+        quantise_w(1)
         transpose(1)
         copy_t(1, ACT)
-        dummies(1, "c")
-        quantise_w(1)
-        multiply(0)
         quantise(1)
         transpose(2)
-        transpose(3)
-        copy_t(2, VEC)
-        copy_t(3, ACT)
-        multiply(1)
-        evac(0, ACT)
+        copy_t(2, ACT)
+        multiply(0)
         quantise(2)
+        transpose(3)
+        copy_t(3, ACT)
+        evac(0, VEC)
+        multiply(1)
+        quantise(3)
         evac(1, ACT)
 
         def drain(t):

@@ -188,7 +188,7 @@ def tile_locallayer_t_kernel(tc, x, W, b, mask, grad_out, out):
 
         transpose(0)
         copy_t(0, ACT)
-        dummies(3, "b")
+        dummies(4, "b")
         group_w(0)
         quantise(0)
         quantise_w(0)
@@ -196,9 +196,11 @@ def tile_locallayer_t_kernel(tc, x, W, b, mask, grad_out, out):
         quantise_w(1)
         transpose(1)
         copy_t(1, ACT)
+        dummies(1, "c")
         quantise(1)
         transpose(2)
         copy_t(2, ACT)
+        dummies(1, "d")
         multiply(0)
         quantise(2)
         transpose(3)

@@ -20,8 +20,7 @@ W_BASE = (0, N - W_SPAN)
 FLOPS = 2 * BATCH * K * N
 BYTES = BATCH * K * 2 + 63488 * 2 + BATCH * N * 4
 
-STEPS = ((2, 2), (4, 2)) + ((2, 2),) * 11
-Q_UNITS = (1, 1, 1, 1) + (2,) * 14
+Q_UNITS = (1, 1, 1, 1, 2, 2) + (2, 1) * 8
 LOADS = (1, 1, 1, 1, 2, 2, 4, 4, 8, 8)
 STORES = (8, 4, 4, 4, 2, 2) + (1,) * 8
 VEC, ACT = 0, 1
@@ -210,28 +209,36 @@ def tile_locallayer_t_kernel(tc, x, W, b, mask, grad_out, out):
         quantise(3)
         evac(1, ACT)
 
-        def drain(t):
-            evac(t, VEC if t % 4 == 0 else ACT)
-
-        t0, m0 = 4, 2
-        waiting = []
-        for i, (n_t, n_m) in enumerate(STEPS):
-            for t in range(t0, t0 + n_t):
+        for a in (4, 6):
+            for t in (a, a + 1):
                 transpose(t)
-            for t in range(t0, t0 + n_t):
-                copy_t(t, VEC if t % 2 == 0 else ACT)
-            if waiting:
-                quantise(waiting.pop(0))
-            waiting.extend(range(t0, t0 + n_t, 2))
-            for t in range(m0, m0 + n_m):
+            copy_t(a, VEC)
+            copy_t(a + 1, ACT)
+            for t in (a - 2, a - 1):
                 multiply(t)
-            for t in range(m0, m0 + n_m):
-                drain(t)
-            while len(waiting) > min(i, 1):
-                quantise(waiting.pop(0))
-            t0, m0 = t0 + n_t, m0 + n_m
-        quantise(waiting[0])
-        for t in range(m0, NT):
+            evac(a - 2, ACT)
+            quantise(a)
+            evac(a - 1, ACT)
+        m_tiles = (6, 7)
+        waiting = ()
+        for a in range(8, NT, 3):
+            for t in range(a, a + 3):
+                transpose(t)
+            copy_t(a, ACT)
+            copy_t(a + 1, VEC)
+            copy_t(a + 2, ACT)
+            for t in waiting:
+                quantise(t)
+            quantise(a)
+            for t in m_tiles:
+                multiply(t)
+            for i, t in enumerate(m_tiles):
+                evac(t, VEC if i == 1 else ACT)
+            m_tiles = range(a, a + 3)
+            waiting = (a + 2,)
+        for t in waiting:
+            quantise(t)
+        for t in m_tiles:
             multiply(t)
-        for t in range(m0, NT):
-            evac(t, VEC if t % 2 == 0 else ACT)
+        for i, t in enumerate(m_tiles):
+            evac(t, ACT if i == 1 else VEC)

@@ -21,7 +21,7 @@ FLOPS = 2 * BATCH * K * N
 BYTES = BATCH * K * 2 + 63488 * 2 + BATCH * N * 4
 
 Q_UNITS = (1, 1, 1, 1, 2, 2) + (2, 1) * 8
-LOADS = (1, 1, 1, 1, 2, 2, 4, 4, 8, 8)
+LOADS = (1, 1, 1, 1, 2, 2, 2, 2, 2, 2, 4, 4, 8)
 STORES = (8, 4, 4, 4, 2, 2) + (1,) * 8
 VEC, ACT = 0, 1
 

from contextlib import ExitStack

import concourse.mybir as mybir
from concourse.masks import make_identity

BF16 = mybir.dt.bfloat16
F32 = mybir.dt.float32
I32 = mybir.dt.int32
U32 = mybir.dt.uint32
U8 = mybir.dt.uint8
E5X4 = mybir.dt.float8_e5m2_x4
E4X4 = mybir.dt.float8_e4m3fn_x4

P = 128
BATCH, K, N = 4096, 1024, 512
NT = BATCH // P
W_SPAN = 320
W_BASE = (0, N - W_SPAN)

FLOPS = 2 * BATCH * K * N
BYTES = BATCH * K * 2 + 63488 * 2 + BATCH * N * 4

Q_UNITS = (1, 1, 1, 1, 2, 2) + (2, 1) * 8
LOADS = (1, 1, 1, 1, 2, 2, 2, 2, 2, 2, 4, 4, 8)
STORES = (8, 4, 4, 4, 2, 2) + (1,) * 8
VEC, ACT = 0, 1


def tile_locallayer_t_kernel(tc, x, W, b, mask, grad_out, out):
    nc = tc.nc
    gx = grad_out.rearrange("(p t) k -> p t k", t=NT)
    ox = out.rearrange("(p t) n -> p t n", t=NT)
    with ExitStack() as ctx:
        const = ctx.enter_context(tc.tile_pool(name="const", bufs=1))
        xin = ctx.enter_context(tc.tile_pool(name="xin", bufs=1))
        grp = ctx.enter_context(tc.tile_pool(name="grp", bufs=10))
        res = ctx.enter_context(tc.tile_pool(name="res", bufs=1))
        psum = ctx.enter_context(tc.psum_pool(name="psum", bufs=1))
        ctx.enter_context(tc.manual_schedule())

        ident = const.tile([P, P], F32, name="ident")
        make_identity(nc, ident[:])
        def w_live(g, u):
            c = 256 * g + 128 * u
            return max(c - 32, 0), min(c + 144, N)

        w_raw = {}
        for g in range(2):
            for u in range(2):
                lo, hi = w_live(g, u)
                w_raw[(g, u)] = const.tile([P, 2, hi - lo], BF16, name="w_raw%d%d" % (g, u))
        w_grp = [const.tile([P, 4 * W_SPAN], BF16, name="w_grp%d" % g, align_bytes=64) for g in range(2)]
        w_codes = const.tile([P, 2 * N], U32, name="w_codes", align_bytes=64)
        w_scales = const.tile([P, 2 * N], U8, name="w_scales", align_bytes=64)
        zeros = const.tile([P, N], BF16, name="zeros")
        nc.vector.memset(zeros[:], 0.0)
        warm = const.tile([P, 8], F32, name="warm")
        warm_out = const.tile([P, 8], F32, name="warm_out")
        nc.vector.memset(warm[:], 0.0)
        nc.scalar.copy(out=warm_out[:], in_=warm[:])
        nc.vector.memset(w_grp[0][:], 0.0)
        nc.vector.memset(w_grp[1][:], 0.0)
        nc.vector.memset(w_codes[:, W_SPAN: N + W_BASE[1]].bitcast(I32), 0)
        nc.vector.memset(w_scales[:, W_SPAN: N + W_BASE[1]].bitcast(I32), 0)

        def dummies(n, tag):
            waste = psum.tile([P, N], F32, name="waste_" + tag, tag="acc3")
            for d in range(n):
                nc.tensor.matmul(waste[:], lhsT=zeros[:, :P], rhs=zeros[:], start=True, stop=True)

        def load_w():
            for g in range(2):
                for u in range(2):
                    r0 = 512 * g + 256 * u
                    lo, hi = w_live(g, u)
                    nc.sync.dma_start(
                        out=w_raw[(g, u)][:],
                        in_=W[r0: r0 + 256, lo:hi].rearrange("(q e) c -> q e c", e=2),
                    )

        x_of = {}
        t0 = 0
        for n in LOADS:
            xt = xin.tile([P, n, K], BF16, name="x%d" % t0)
            nc.sync.dma_start(out=xt[:], in_=gx[:, t0: t0 + n, :])
            if t0 == 0:
                load_w()
            for j in range(n):
                x_of[t0 + j] = xt[:, j, :]
            t0 += n
        o_of = {}
        store_after = {}
        t0 = 0
        for n in STORES:
            ot = res.tile([P, n, N], F32, name="o%d" % t0)
            for j in range(n):
                o_of[t0 + j] = ot[:, j, :]
            store_after[t0 + n - 1] = (ot, t0, n)
            t0 += n

        dummies(4, "a")

        def group_w(g):
            for u in range(2):
                lo, hi = w_live(g, u)
                dst = w_grp[g][:].rearrange("p (c t) -> p c t", t=4)[:, lo - W_BASE[g]: hi - W_BASE[g], 2 * u: 2 * u + 2]
                src = w_raw[(g, u)][:].rearrange("p e c -> p c e")
                if g == 0 or u == 1:
                    nc.vector.tensor_copy(out=dst, in_=src)
                else:
                    nc.scalar.copy(out=dst, in_=src)

        def quantise_w(g):
            cuts = ((0, 256, 320), (0, 64, 320))[g]
            for lo, hi in zip(cuts[:-1], cuts[1:]):
                c0 = N * g + W_BASE[g]
                nc.vector.quantize_mx(
                    out=w_codes[:, c0 + lo: c0 + hi].bitcast(E4X4),
                    scales=w_scales[:, c0 + lo: c0 + hi],
                    in_=w_grp[g][:, 4 * lo: 4 * hi],
                )

        def firsts(sizes):
            return [sum(sizes[:i]) for i in range(len(sizes))]

        q_first = firsts(Q_UNITS)
        unit_of = {}
        for iq in range(len(Q_UNITS)):
            for j in range(Q_UNITS[iq]):
                unit_of[q_first[iq] + j] = (iq, j)
        banks = {}
        units = {}

        def copy(eng, dst, src):
            if eng == VEC:
                nc.vector.tensor_copy(out=dst, in_=src)
            else:
                nc.scalar.copy(out=dst, in_=src)

        def transpose(t):
            tp = psum.tile([P, 4, P], F32, name="tp%d" % t, tag="tp%d" % (t % 4))
            words = x_of[t].bitcast(F32)
            for q in range(4):
                nc.tensor.transpose(tp[:, q, :], words[:, P * q: P * (q + 1)], ident[:])
            banks[t] = tp

        def copy_t(t, eng):
            iq, j = unit_of[t]
            if iq not in units:
                n = Q_UNITS[iq]
                grouped = grp.tile([P, n * K], BF16, name="grouped%d" % iq, tag="grouped", align_bytes=64)
                codes = grp.tile([P, n * K // 4], U32, name="codes%d" % iq, tag="codes", align_bytes=64)
                scales = grp.tile([P, n * K // 4], U8, name="scales%d" % iq, tag="scales", align_bytes=64)
                units[iq] = (grouped, codes, scales)
            grouped = units[iq][0]
            dst = grouped[:, K * j: K * (j + 1)].bitcast(F32).rearrange("p (g c u) -> p g c u", g=2, u=2)
            copy(eng, dst, banks[t][:].rearrange("p (g u) c -> p g c u", u=2))

        def quantise(t):
            grouped, codes, scales = units[unit_of[t][0]]
            nc.vector.quantize_mx(out=codes[:].bitcast(E5X4), scales=scales[:], in_=grouped[:])

        accs = {}

        def multiply(t):
            iq, j = unit_of[t]
            grouped, codes, scales = units[iq]
            acc = psum.tile([P, N], F32, name="acc%d" % t, tag="acc%d" % (t % 4))
            for g in range(2):
                c0 = 256 * j + P * g
                nc.tensor.matmul_mx(
                    out=acc[:],
                    lhsT=codes[:, c0: c0 + P].bitcast(E5X4),
                    lhsT_scale=scales[:, c0: c0 + P],
                    rhs=w_codes[:, N * g: N * (g + 1)].bitcast(E4X4),
                    rhs_scale=w_scales[:, N * g: N * (g + 1)],
                    start=(g == 0),
                    stop=(g == 1),
                )
            accs[t] = acc

        def evac(t, eng):
            copy(eng, o_of[t], accs[t][:])
            if t in store_after:
                ot, s0, n = store_after[t]
                nc.sync.dma_start(out=ox[:, s0: s0 + n, :], in_=ot[:])

        transpose(0)
        copy_t(0, ACT)
        dummies(4, "b")
        group_w(0)
        quantise(0)
        quantise_w(0)
        group_w(1)
        quantise_w(1)
        transpose(1)
        copy_t(1, ACT)
        dummies(1, "c")
        quantise(1)
        transpose(2)
        copy_t(2, ACT)
        dummies(1, "d")
        multiply(0)
        quantise(2)
        transpose(3)
        copy_t(3, ACT)
        evac(0, VEC)
        multiply(1)
        quantise(3)
        evac(1, ACT)

        for a in (4, 6):
            for t in (a, a + 1):
                transpose(t)
            copy_t(a, VEC)
            copy_t(a + 1, ACT)
            for t in (a - 2, a - 1):
                multiply(t)
            evac(a - 2, ACT)
            quantise(a)
            evac(a - 1, ACT)
        m_tiles = (6, 7)
        waiting = ()
        for a in range(8, NT, 3):
            for t in range(a, a + 3):
                transpose(t)
            copy_t(a, ACT)
            copy_t(a + 1, VEC)
            copy_t(a + 2, ACT)
            for t in waiting:
                quantise(t)
            quantise(a)
            for t in m_tiles:
                multiply(t)
            for i, t in enumerate(m_tiles):
                evac(t, VEC if i == 1 else ACT)
            m_tiles = range(a, a + 3)
            waiting = (a + 2,)
        for t in waiting:
            quantise(t)
        for t in m_tiles:
            multiply(t)
        for i, t in enumerate(m_tiles):
            evac(t, ACT if i == 1 else VEC)
